import numpy as np
import ml_dtypes


def mxq(x, axis, fmt="e4m3"):
    dtype, down = {"e4m3": (ml_dtypes.float8_e4m3fn, 7), "e5m2": (ml_dtypes.float8_e5m2, 14)}[fmt]
    v = np.moveaxis(np.asarray(x, np.float32).astype(ml_dtypes.bfloat16).astype(np.float64), axis, -1)
    blocks = v.reshape(v.shape[:-1] + (-1, 32))
    amax = np.abs(blocks).max(-1, keepdims=True)
    byte = np.maximum(np.where(amax > 0, np.frexp(amax)[1] - 1 + 127, 0) - down, 1)
    scale = np.exp2(byte - 127.0)
    codes = (blocks / scale).astype(np.float32).astype(dtype).astype(np.float64)
    return np.moveaxis((codes * scale).reshape(v.shape), -1, axis)


WIDE = False


def mx_kscale(k):
    if not WIDE:
        return np.ones(k)
    levels = np.array([10, -10, 5, -5, 0])
    a = np.random.permutation(np.resize(levels, k // 512 * 4)).reshape(k // 512, 4)
    idx = np.arange(k)
    return np.exp2(a[idx // 512, idx % 128 // 32])


BF16 = ml_dtypes.bfloat16


def bf(x):
    return np.asarray(x, np.float32).astype(BF16)


def f64(x):
    return np.asarray(x).astype(np.float64)


E2M1 = np.array([0.0, 0.5, 1.0, 1.5, 2.0, 3.0, 4.0, 6.0, -0.0, -0.5, -1.0, -1.5, -2.0, -3.0, -4.0, -6.0])


def pack_weight(w, fmt):
    k, n = w.shape
    w = f64(bf(w)).reshape(k // 32, 32, n)
    amax = np.abs(w).max(1)
    if fmt == "e4m3":
        byte = np.frexp(amax)[1] - 1 + 127 - 7
    else:
        mant, ex = np.frexp(amax / 6.0)
        byte = np.where(mant > 0.5, ex, ex - 1) + 127
    byte = np.clip(np.where(amax > 0, byte, 1), 1, 254)
    scaled = (w * np.exp2(127.0 - byte)[:, None, :]).reshape(k, n).astype(np.float32)
    by_word = np.ascontiguousarray(scaled.reshape(k // 512, 128, 4, n).transpose(0, 1, 3, 2))
    if fmt == "e4m3":
        words = by_word.astype(ml_dtypes.float8_e4m3fn).view(np.uint8)
    else:
        c = by_word.astype(ml_dtypes.float4_e2m1fn).view(np.uint8) & 0xF
        words = c[..., 0::2] | (c[..., 1::2] << 4)
    return np.ascontiguousarray(words), np.ascontiguousarray(byte.astype(np.uint8).reshape(k // 512, 16, n))


def unpack_weight(words, scales, fmt):
    g, p, n, _ = words.shape
    if fmt == "e4m3":
        vals = np.ascontiguousarray(words).view(ml_dtypes.float8_e4m3fn).astype(np.float64)
    else:
        nib = np.empty((g, p, n, 4), np.uint8)
        nib[..., 0::2] = words & 0xF
        nib[..., 1::2] = words >> 4
        vals = E2M1[nib]
    vals = vals * np.repeat(np.exp2(scales.astype(np.float64) - 127.0), 8, axis=1)[..., None]
    return vals.transpose(0, 1, 3, 2).reshape(g * 512, n)


B, IN_DIM, MEM = 2048, 3840, 256
DIN = MEM + IN_DIM
F = 2 * MEM
LN_EPS = 1e-5
FMT = "e4m3"


def erf(v):
    a = np.minimum(np.abs(v), 6.0)
    a2 = 2.0 * a * a
    term = a.copy()
    tot = a.copy()
    for n in range(1, 120):
        term = term * a2 / (2 * n + 1)
        tot = tot + term
    return np.sign(v) * (2.0 / np.sqrt(np.pi)) * np.exp(-a * a) * tot


def gelu_erf(v):
    return 0.5 * v * (1.0 + erf(v / np.sqrt(2.0)))


def layernorm(t, g, b):
    mu = t.mean(-1, keepdims=True)
    var = np.square(t - mu).mean(-1, keepdims=True)
    return (t - mu) / np.sqrt(var + LN_EPS) * g + b


def setup_inputs():
    s = mx_kscale(DIN)
    x = bf(np.random.standard_normal((B, IN_DIM)) * s[MEM:])
    h = bf(np.random.standard_normal((B, MEM)) * s[:MEM])
    W1_words, W1_scales = pack_weight(np.random.standard_normal((DIN, F)) * 1.3 / np.sqrt(DIN) / s[:, None], FMT)
    b1 = bf(np.random.standard_normal(F) * 0.3)
    g1 = bf(1.0 + 0.1 * np.random.standard_normal(F))
    be1 = bf(np.random.standard_normal(F) * 0.2)
    W2_words, W2_scales = pack_weight(np.random.standard_normal((F, MEM)) / np.sqrt(F), FMT)
    b2 = bf(np.random.standard_normal(MEM) * 0.2)
    return {"x": x,
            "h": h,
            "W1_words": W1_words,
            "W1_scales": W1_scales,
            "b1": b1,
            "g1": g1,
            "be1": be1,
            "W2_words": W2_words,
            "W2_scales": W2_scales,
            "b2": b2}


def reference(x, h, W1_words, W1_scales, b1, g1, be1, W2_words, W2_scales, b2):
    combined = np.concatenate([f64(h), f64(x)], axis=-1)
    u = (mxq(combined, 1, "e4m3") @ unpack_weight(W1_words, W1_scales, FMT)) + f64(b1)
    t = gelu_erf(layernorm(u, f64(g1), f64(be1)))
    return np.tanh((mxq(t, 1, "e4m3") @ unpack_weight(W2_words, W2_scales, FMT)) + f64(b2))

@@ -1,0 +1,334 @@
+from contextlib import ExitStack
+
+import concourse.mybir as mybir
+from concourse.masks import make_identity
+
+F32 = mybir.dt.float32
+BF16 = mybir.dt.bfloat16
+I32 = mybir.dt.int32
+U32 = mybir.dt.uint32
+U8 = mybir.dt.uint8
+FP8X4 = mybir.dt.float8_e4m3fn_x4
+ACT = mybir.ActivationFunctionType
+ALU = mybir.AluOpType
+
+P = 128
+PACK = 4
+WORDS = 2
+K_PASS = P * PACK
+
+B, IN_DIM, MEM = 2048, 3840, 256
+DIN = MEM + IN_DIM
+F = 2 * MEM
+LN_EPS = 1e-5
+
+ROW_TILES = B // P
+PASSES = DIN // K_PASS
+HALF_PASSES = PASSES // 2
+K_HALF = HALF_PASSES * K_PASS
+BANK_PASSES = 2
+QUADRANTS = 4
+
+LOAD_AHEAD = 6
+
+FLOPS = 2 * B * DIN * F + 2 * B * F * MEM
+
+
+def tile_liquidmemorycell_pa_kernel(
+    tc, x, h, W1_words, W1_scales, b1, g1, be1, W2_words, W2_scales, b2, out
+):
+    nc = tc.nc
+    with ExitStack() as ctx:
+        ctx.enter_context(tc.manual_schedule())
+        const = ctx.enter_context(tc.tile_pool(name="const", bufs=1))
+        raw_pool = ctx.enter_context(tc.tile_pool(name="raw", bufs=2 * LOAD_AHEAD))
+        half_pool = ctx.enter_context(tc.tile_pool(name="half", bufs=4))
+        work = ctx.enter_context(tc.tile_pool(name="work", bufs=3))
+        stat = ctx.enter_context(tc.tile_pool(name="stat", bufs=4))
+        c_psum = ctx.enter_context(tc.psum_pool(name="c_psum", bufs=4))
+        u_psum = ctx.enter_context(tc.psum_pool(name="u_psum", bufs=2))
+        z_psum = ctx.enter_context(tc.psum_pool(name="z_psum", bufs=1))
+        o_psum = ctx.enter_context(tc.psum_pool(name="o_psum", bufs=1))
+
+        bias_row = const.tile([P, F + MEM], BF16)
+        nc.vector.memset(bias_row[:], 0.0)
+        nc.scalar.dma_start(out=bias_row[0:1, 0:F], in_=b1.rearrange("(o f) -> o f", o=1))
+        nc.scalar.dma_start(out=bias_row[0:1, F : F + MEM], in_=b2.rearrange("(o f) -> o f", o=1))
+        g1_bf = const.tile([P, PACK], BF16)
+        be1_bf = const.tile([P, PACK], BF16)
+        nc.scalar.dma_start(out=g1_bf[:], in_=g1.rearrange("(q t) -> q t", t=PACK))
+        nc.scalar.dma_start(out=be1_bf[:], in_=be1.rearrange("(q t) -> q t", t=PACK))
+
+        ones = const.tile([P, P], BF16)
+        nc.vector.memset(ones[:], 1.0)
+        neg_half = const.tile([P, 1], F32)
+        nc.vector.memset(neg_half[:], -0.5)
+        identity = const.tile([P, P], F32)
+        make_identity(nc, identity[:])
+
+        table_warmer = const.tile([P, 1], F32)
+        nc.scalar.activation(out=table_warmer[:], in_=neg_half[:], func=ACT.Gelu)
+
+        w1_codes = const.tile([P, PASSES, PACK * F], U8, align_bytes=64)
+        w1_scales = const.tile([P, PASSES, F], U8, align_bytes=64)
+        w2_codes = const.tile([P, PACK * MEM], U8, align_bytes=64)
+        w2_scales = const.tile([P, MEM], U8, align_bytes=64)
+        nc.vector.memset(w1_scales[:].bitcast(I32), 0)
+        nc.vector.memset(w2_scales[:].bitcast(I32), 0)
+
+        raw = {}
+
+        def load_rows(i):
+            rows = slice(i * P, (i + 1) * P)
+            for s in range(2):
+                c_raw = raw_pool.tile([P, K_HALF], BF16)
+                if s == 0:
+                    nc.sync.dma_start(out=c_raw[:, 0:MEM], in_=h[rows, :])
+                    nc.sync.dma_start(out=c_raw[:, MEM:K_HALF], in_=x[rows, 0 : K_HALF - MEM])
+                else:
+                    nc.sync.dma_start(out=c_raw[:], in_=x[rows, K_HALF - MEM : IN_DIM])
+                raw[(i, s)] = c_raw
+
+        load_rows(0)
+        load_rows(1)
+        for quad in range(QUADRANTS):
+            nc.sync.dma_start(
+                out=w1_scales[32 * quad : 32 * quad + 4, :, :].bitcast(I32),
+                in_=W1_scales[:, 4 * quad : 4 * quad + 4, :].rearrange("g r n -> r g n").bitcast(I32),
+            )
+        for g in range(PASSES):
+            nc.sync.dma_start(
+                out=w1_codes[:, g, :].bitcast(I32),
+                in_=W1_words[g].rearrange("q n t -> q (n t)").bitcast(I32),
+            )
+        nc.sync.dma_start(
+            out=w2_codes[:].bitcast(I32),
+            in_=W2_words[0].rearrange("q n t -> q (n t)").bitcast(I32),
+        )
+        for quad in range(QUADRANTS):
+            nc.sync.dma_start(
+                out=w2_scales[32 * quad : 32 * quad + 4, :].bitcast(I32),
+                in_=W2_scales[0, 4 * quad : 4 * quad + 4, :].bitcast(I32),
+            )
+        for i in range(2, LOAD_AHEAD - 2):
+            load_rows(i)
+
+        b1_rows = const.tile([P, PACK, P], F32)
+        b2_rows = const.tile([P, MEM], F32)
+        gain = const.tile([P, PACK], F32)
+        shift = const.tile([P, PACK], F32)
+
+        def spread_small_vectors():
+            acc = u_psum.tile([P, F], F32)
+            nc.tensor.matmul(out=acc[:], lhsT=ones[:], rhs=bias_row[:, 0:F], start=True, stop=True)
+            nc.scalar.copy(out=b1_rows[:], in_=acc[:].rearrange("r (q t) -> r t q", t=PACK))
+            acc2 = o_psum.tile([P, MEM], F32)
+            nc.tensor.matmul(
+                out=acc2[:], lhsT=ones[:], rhs=bias_row[:, F : F + MEM], start=True, stop=True
+            )
+            nc.scalar.copy(out=b2_rows[:], in_=acc2[:])
+            nc.gpsimd.tensor_copy(out=gain[:], in_=g1_bf[:])
+            nc.gpsimd.tensor_copy(out=shift[:], in_=be1_bf[:])
+
+        ordered = {}
+        side_by_side = {}
+        c_mx = {}
+        u_banks = {}
+        u_rows = {}
+        row_sums = {}
+        neg_means = {}
+        rstds = {}
+        z_rows = {}
+        z_banks = {}
+        t_planes = {}
+        t_words = {}
+        t_mx = {}
+        o_banks = {}
+        o_rows = {}
+
+        def sort_words(i, s):
+            c_sorted = half_pool.tile([P, HALF_PASSES, WORDS, P], F32)
+            nc.vector.tensor_copy(
+                out=c_sorted[:],
+                in_=raw[(i, s)][:]
+                .bitcast(F32)
+                .rearrange("r (g q w) -> r g w q", g=HALF_PASSES, w=WORDS),
+            )
+            ordered[(i, s)] = c_sorted
+
+        def transpose_half(i, s):
+            grouped = half_pool.tile([P, HALF_PASSES, P, PACK], BF16, align_bytes=64)
+            for first in range(0, HALF_PASSES, BANK_PASSES):
+                bank = c_psum.tile([P, BANK_PASSES, WORDS, P], F32)
+                for g in range(BANK_PASSES):
+                    for w in range(WORDS):
+                        nc.tensor.transpose(
+                            bank[:, g, w, :], ordered[(i, s)][:, first + g, w, :], identity[:]
+                        )
+                nc.scalar.copy(
+                    out=grouped[:, first : first + BANK_PASSES, :, :].bitcast(F32),
+                    in_=bank[:].rearrange("q g w r -> q g r w"),
+                )
+            side_by_side[(i, s)] = grouped
+
+        def quantise_half(i, s):
+            c_codes = half_pool.tile([P, HALF_PASSES, P], U32, align_bytes=64)
+            c_scales = half_pool.tile([P, HALF_PASSES, P], U8, align_bytes=64)
+            nc.vector.quantize_mx(
+                out=c_codes[:].rearrange("q g r -> q (g r)").bitcast(FP8X4),
+                scales=c_scales[:].rearrange("q g r -> q (g r)"),
+                in_=side_by_side[(i, s)][:].rearrange("q g r t -> q (g r t)"),
+            )
+            c_mx[(i, s)] = (c_codes, c_scales)
+
+        def first_matmul(i):
+            acc = u_psum.tile([P, F], F32)
+            for g in range(PASSES):
+                c_codes, c_scales = c_mx[(i, g // HALF_PASSES)]
+                nc.tensor.matmul_mx(
+                    out=acc[:],
+                    lhsT=c_codes[:, g % HALF_PASSES, :].bitcast(FP8X4),
+                    lhsT_scale=c_scales[:, g % HALF_PASSES, :],
+                    rhs=w1_codes[:, g, :].bitcast(FP8X4),
+                    rhs_scale=w1_scales[:, g, :],
+                    start=(g == 0),
+                    stop=(g == PASSES - 1),
+                )
+            u_banks[i] = acc
+
+        def add_bias_and_sum(i):
+            u = work.tile([P, PACK, P], F32)
+            row_sum = stat.tile([P, 1], F32)
+            nc.vector.scalar_tensor_tensor(
+                out=u[:],
+                in0=u_banks[i][:].rearrange("r (q t) -> r t q", t=PACK),
+                scalar=1.0,
+                in1=b1_rows[:],
+                op0=ALU.mult,
+                op1=ALU.add,
+                accum_out=row_sum[:],
+            )
+            u_rows[i] = u
+            row_sums[i] = row_sum
+
+        def variance(i):
+            neg_mean = stat.tile([P, 1], F32)
+            nc.vector.tensor_scalar(
+                out=neg_mean[:], in0=row_sums[i][:], scalar1=-1.0 / F, scalar2=None, op0=ALU.mult
+            )
+            neg_means[i] = neg_mean
+            squares = work.tile([P, F], BF16)
+            sq_sum = stat.tile([P, 1], F32)
+            nc.scalar.activation(
+                out=squares[:],
+                in_=u_rows[i][:].rearrange("r t q -> r (t q)"),
+                func=ACT.Square,
+                bias=neg_mean[:],
+                scale=1.0,
+                accum_out=sq_sum[:],
+            )
+            var_eps = stat.tile([P, 1], F32)
+            nc.gpsimd.tensor_scalar(
+                out=var_eps[:], in0=sq_sum[:], scalar1=1.0 / F, scalar2=LN_EPS, op0=ALU.mult, op1=ALU.add
+            )
+            rstd = stat.tile([P, 1], F32)
+            nc.gpsimd.tensor_tensor(out=rstd[:], in0=var_eps[:], in1=neg_half[:], op=ALU.pow)
+            rstds[i] = rstd
+
+        def normalise(i):
+            z = work.tile([P, PACK, P], F32)
+            nc.vector.tensor_scalar(
+                out=z[:],
+                in0=u_rows[i][:],
+                scalar1=neg_means[i][:],
+                scalar2=rstds[i][:],
+                op0=ALU.add,
+                op1=ALU.mult,
+            )
+            z_rows[i] = z
+
+        def transpose_normalised(i):
+            z_bank = z_psum.tile([P, PACK, P], F32)
+            for t in range(PACK):
+                nc.tensor.transpose(z_bank[:, t, :], z_rows[i][:, t, :], identity[:])
+            z_banks[i] = z_bank
+
+        def gelu(i):
+            t_plane = work.tile([P, PACK, P], BF16)
+            for t in range(PACK):
+                nc.scalar.activation(
+                    out=t_plane[:, t, :],
+                    in_=z_banks[i][:, t, :],
+                    func=ACT.Gelu,
+                    scale=gain[:, t : t + 1],
+                    bias=shift[:, t : t + 1],
+                )
+            t_planes[i] = t_plane
+
+        def regroup_t(i):
+            t_grouped = work.tile([P, P, PACK], BF16, align_bytes=64)
+            nc.vector.tensor_copy(out=t_grouped[:], in_=t_planes[i][:].rearrange("q t r -> q r t"))
+            t_words[i] = t_grouped
+
+        def quantise_t(i):
+            t_codes = work.tile([P, P], U32, align_bytes=64)
+            t_scales = work.tile([P, P], U8, align_bytes=64)
+            nc.vector.quantize_mx(
+                out=t_codes[:].bitcast(FP8X4),
+                scales=t_scales[:],
+                in_=t_words[i][:].rearrange("q r t -> q (r t)"),
+            )
+            t_mx[i] = (t_codes, t_scales)
+
+        def second_matmul(i):
+            t_codes, t_scales = t_mx[i]
+            acc2 = o_psum.tile([P, MEM], F32)
+            nc.tensor.matmul_mx(
+                out=acc2[:],
+                lhsT=t_codes[:].bitcast(FP8X4),
+                lhsT_scale=t_scales[:],
+                rhs=w2_codes[:].bitcast(FP8X4),
+                rhs_scale=w2_scales[:],
+                start=True,
+                stop=True,
+            )
+            o_banks[i] = acc2
+
+        def add_second_bias(i):
+            o = work.tile([P, MEM], F32)
+            nc.vector.tensor_tensor(out=o[:], in0=o_banks[i][:], in1=b2_rows[:], op=ALU.add)
+            o_rows[i] = o
+
+        def tanh_and_store(i):
+            nc.scalar.activation(out=o_rows[i][:], in_=o_rows[i][:], func=ACT.Tanh)
+            nc.sync.dma_start(out=out[i * P : (i + 1) * P, :], in_=o_rows[i][:])
+
+        def run(stage, i, *half):
+            if 0 <= i < ROW_TILES:
+                stage(i, *half)
+
+        def step(j):
+            run(load_rows, j + LOAD_AHEAD)
+            run(add_bias_and_sum, j - 1)
+            run(quantise_t, j - 4)
+            run(transpose_half, j + 1, 0)
+            run(variance, j - 1)
+            run(transpose_half, j + 1, 1)
+            run(transpose_normalised, j - 3)
+            run(sort_words, j + 2, 0)
+            run(sort_words, j + 2, 1)
+            run(second_matmul, j - 4)
+            run(first_matmul, j)
+            run(add_second_bias, j - 4)
+            run(normalise, j - 2)
+            run(quantise_half, j + 1, 0)
+            run(gelu, j - 3)
+            run(quantise_half, j + 1, 1)
+            run(tanh_and_store, j - 4)
+            run(regroup_t, j - 3)
+
+        step(-2)
+        step(-1)
+        spread_small_vectors()
+        for j in range(ROW_TILES + 4):
+            step(j)

@@ -30,6 +30,7 @@ BANK_PASSES = 2
 QUADRANTS = 4
 
 LOAD_AHEAD = 6
+TILES_BEFORE_W1 = 2
 
 FLOPS = 2 * B * DIN * F + 2 * B * F * MEM
 
@@ -89,8 +90,8 @@ def tile_liquidmemorycell_pa_kernel(
                     nc.sync.dma_start(out=c_raw[:], in_=x[rows, K_HALF - MEM : IN_DIM])
                 raw[(i, s)] = c_raw
 
-        load_rows(0)
-        load_rows(1)
+        for i in range(TILES_BEFORE_W1):
+            load_rows(i)
         for quad in range(QUADRANTS):
             nc.sync.dma_start(
                 out=w1_scales[32 * quad : 32 * quad + 4, :, :].bitcast(I32),
@@ -101,6 +102,8 @@ def tile_liquidmemorycell_pa_kernel(
                 out=w1_codes[:, g, :].bitcast(I32),
                 in_=W1_words[g].rearrange("q n t -> q (n t)").bitcast(I32),
             )
+        for i in range(TILES_BEFORE_W1, LOAD_AHEAD - 2):
+            load_rows(i)
         nc.sync.dma_start(
             out=w2_codes[:].bitcast(I32),
             in_=W2_words[0].rearrange("q n t -> q (n t)").bitcast(I32),
@@ -110,8 +113,6 @@ def tile_liquidmemorycell_pa_kernel(
                 out=w2_scales[32 * quad : 32 * quad + 4, :].bitcast(I32),
                 in_=W2_scales[0, 4 * quad : 4 * quad + 4, :].bitcast(I32),
             )
-        for i in range(2, LOAD_AHEAD - 2):
-            load_rows(i)
 
         b1_rows = const.tile([P, PACK, P], F32)
         b2_rows = const.tile([P, MEM], F32)
@@ -307,18 +308,25 @@ def tile_liquidmemorycell_pa_kernel(
             if 0 <= i < ROW_TILES:
                 stage(i, *half)
 
+        def multiply(j):
+            run(second_matmul, j - 4)
+            run(first_matmul, j)
+
         def step(j):
+            multiply_first = j + 1 == TILES_BEFORE_W1
             run(load_rows, j + LOAD_AHEAD)
             run(add_bias_and_sum, j - 1)
             run(quantise_t, j - 4)
+            if multiply_first:
+                multiply(j)
             run(transpose_half, j + 1, 0)
             run(variance, j - 1)
             run(transpose_half, j + 1, 1)
             run(transpose_normalised, j - 3)
             run(sort_words, j + 2, 0)
             run(sort_words, j + 2, 1)
-            run(second_matmul, j - 4)
-            run(first_matmul, j)
+            if not multiply_first:
+                multiply(j)
             run(add_second_bias, j - 4)
             run(normalise, j - 2)
             run(quantise_half, j + 1, 0)

@@ -29,8 +29,8 @@ K_HALF = HALF_PASSES * K_PASS
 BANK_PASSES = 2
 QUADRANTS = 4
 
-LOAD_AHEAD = 6
 TILES_BEFORE_W1 = 2
+LOAD_AHEAD = 6
 
 FLOPS = 2 * B * DIN * F + 2 * B * F * MEM
 
@@ -49,7 +49,7 @@ def tile_liquidmemorycell_pa_kernel(
         c_psum = ctx.enter_context(tc.psum_pool(name="c_psum", bufs=4))
         u_psum = ctx.enter_context(tc.psum_pool(name="u_psum", bufs=2))
         z_psum = ctx.enter_context(tc.psum_pool(name="z_psum", bufs=1))
-        o_psum = ctx.enter_context(tc.psum_pool(name="o_psum", bufs=1))
+        y_psum = ctx.enter_context(tc.psum_pool(name="y_psum", bufs=1))
 
         bias_row = const.tile([P, F + MEM], BF16)
         nc.vector.memset(bias_row[:], 0.0)
@@ -57,8 +57,8 @@ def tile_liquidmemorycell_pa_kernel(
         nc.scalar.dma_start(out=bias_row[0:1, F : F + MEM], in_=b2.rearrange("(o f) -> o f", o=1))
         g1_bf = const.tile([P, PACK], BF16)
         be1_bf = const.tile([P, PACK], BF16)
-        nc.scalar.dma_start(out=g1_bf[:], in_=g1.rearrange("(q t) -> q t", t=PACK))
-        nc.scalar.dma_start(out=be1_bf[:], in_=be1.rearrange("(q t) -> q t", t=PACK))
+        nc.scalar.dma_start(out=g1_bf[:], in_=g1.rearrange("(q e) -> q e", e=PACK))
+        nc.scalar.dma_start(out=be1_bf[:], in_=be1.rearrange("(q e) -> q e", e=PACK))
 
         ones = const.tile([P, P], BF16)
         nc.vector.memset(ones[:], 1.0)
@@ -100,13 +100,13 @@ def tile_liquidmemorycell_pa_kernel(
         for g in range(PASSES):
             nc.sync.dma_start(
                 out=w1_codes[:, g, :].bitcast(I32),
-                in_=W1_words[g].rearrange("q n t -> q (n t)").bitcast(I32),
+                in_=W1_words[g].rearrange("q n e -> q (n e)").bitcast(I32),
             )
         for i in range(TILES_BEFORE_W1, LOAD_AHEAD - 2):
             load_rows(i)
         nc.sync.dma_start(
             out=w2_codes[:].bitcast(I32),
-            in_=W2_words[0].rearrange("q n t -> q (n t)").bitcast(I32),
+            in_=W2_words[0].rearrange("q n e -> q (n e)").bitcast(I32),
         )
         for quad in range(QUADRANTS):
             nc.sync.dma_start(
@@ -120,14 +120,14 @@ def tile_liquidmemorycell_pa_kernel(
         shift = const.tile([P, PACK], F32)
 
         def spread_small_vectors():
-            acc = u_psum.tile([P, F], F32)
-            nc.tensor.matmul(out=acc[:], lhsT=ones[:], rhs=bias_row[:, 0:F], start=True, stop=True)
-            nc.scalar.copy(out=b1_rows[:], in_=acc[:].rearrange("r (q t) -> r t q", t=PACK))
-            acc2 = o_psum.tile([P, MEM], F32)
+            u_bank = u_psum.tile([P, F], F32)
+            nc.tensor.matmul(out=u_bank[:], lhsT=ones[:], rhs=bias_row[:, 0:F], start=True, stop=True)
+            nc.scalar.copy(out=b1_rows[:], in_=u_bank[:].rearrange("r (q e) -> r e q", e=PACK))
+            y_bank = y_psum.tile([P, MEM], F32)
             nc.tensor.matmul(
-                out=acc2[:], lhsT=ones[:], rhs=bias_row[:, F : F + MEM], start=True, stop=True
+                out=y_bank[:], lhsT=ones[:], rhs=bias_row[:, F : F + MEM], start=True, stop=True
             )
-            nc.scalar.copy(out=b2_rows[:], in_=acc2[:])
+            nc.scalar.copy(out=b2_rows[:], in_=y_bank[:])
             nc.gpsimd.tensor_copy(out=gain[:], in_=g1_bf[:])
             nc.gpsimd.tensor_copy(out=shift[:], in_=be1_bf[:])
 
@@ -144,8 +144,8 @@ def tile_liquidmemorycell_pa_kernel(
         t_planes = {}
         t_words = {}
         t_mx = {}
-        o_banks = {}
-        o_rows = {}
+        y_banks = {}
+        y_rows = {}
 
         def sort_words(i, s):
             c_sorted = half_pool.tile([P, HALF_PASSES, WORDS, P], F32)
@@ -160,15 +160,15 @@ def tile_liquidmemorycell_pa_kernel(
         def transpose_half(i, s):
             grouped = half_pool.tile([P, HALF_PASSES, P, PACK], BF16, align_bytes=64)
             for first in range(0, HALF_PASSES, BANK_PASSES):
-                bank = c_psum.tile([P, BANK_PASSES, WORDS, P], F32)
+                c_bank = c_psum.tile([P, BANK_PASSES, WORDS, P], F32)
                 for g in range(BANK_PASSES):
                     for w in range(WORDS):
                         nc.tensor.transpose(
-                            bank[:, g, w, :], ordered[(i, s)][:, first + g, w, :], identity[:]
+                            c_bank[:, g, w, :], ordered[(i, s)][:, first + g, w, :], identity[:]
                         )
                 nc.scalar.copy(
                     out=grouped[:, first : first + BANK_PASSES, :, :].bitcast(F32),
-                    in_=bank[:].rearrange("q g w r -> q g r w"),
+                    in_=c_bank[:].rearrange("q g w r -> q g r w"),
                 )
             side_by_side[(i, s)] = grouped
 
@@ -178,16 +178,16 @@ def tile_liquidmemorycell_pa_kernel(
             nc.vector.quantize_mx(
                 out=c_codes[:].rearrange("q g r -> q (g r)").bitcast(FP8X4),
                 scales=c_scales[:].rearrange("q g r -> q (g r)"),
-                in_=side_by_side[(i, s)][:].rearrange("q g r t -> q (g r t)"),
+                in_=side_by_side[(i, s)][:].rearrange("q g r e -> q (g r e)"),
             )
             c_mx[(i, s)] = (c_codes, c_scales)
 
         def first_matmul(i):
-            acc = u_psum.tile([P, F], F32)
+            u_bank = u_psum.tile([P, F], F32)
             for g in range(PASSES):
                 c_codes, c_scales = c_mx[(i, g // HALF_PASSES)]
                 nc.tensor.matmul_mx(
-                    out=acc[:],
+                    out=u_bank[:],
                     lhsT=c_codes[:, g % HALF_PASSES, :].bitcast(FP8X4),
                     lhsT_scale=c_scales[:, g % HALF_PASSES, :],
                     rhs=w1_codes[:, g, :].bitcast(FP8X4),
@@ -195,14 +195,14 @@ def tile_liquidmemorycell_pa_kernel(
                     start=(g == 0),
                     stop=(g == PASSES - 1),
                 )
-            u_banks[i] = acc
+            u_banks[i] = u_bank
 
         def add_bias_and_sum(i):
             u = work.tile([P, PACK, P], F32)
             row_sum = stat.tile([P, 1], F32)
             nc.vector.scalar_tensor_tensor(
                 out=u[:],
-                in0=u_banks[i][:].rearrange("r (q t) -> r t q", t=PACK),
+                in0=u_banks[i][:].rearrange("r (q e) -> r e q", e=PACK),
                 scalar=1.0,
                 in1=b1_rows[:],
                 op0=ALU.mult,
@@ -222,7 +222,7 @@ def tile_liquidmemorycell_pa_kernel(
             sq_sum = stat.tile([P, 1], F32)
             nc.scalar.activation(
                 out=squares[:],
-                in_=u_rows[i][:].rearrange("r t q -> r (t q)"),
+                in_=u_rows[i][:].rearrange("r e q -> r (e q)"),
                 func=ACT.Square,
                 bias=neg_mean[:],
                 scale=1.0,
@@ -250,25 +250,25 @@ def tile_liquidmemorycell_pa_kernel(
 
         def transpose_normalised(i):
             z_bank = z_psum.tile([P, PACK, P], F32)
-            for t in range(PACK):
-                nc.tensor.transpose(z_bank[:, t, :], z_rows[i][:, t, :], identity[:])
+            for e in range(PACK):
+                nc.tensor.transpose(z_bank[:, e, :], z_rows[i][:, e, :], identity[:])
             z_banks[i] = z_bank
 
         def gelu(i):
             t_plane = work.tile([P, PACK, P], BF16)
-            for t in range(PACK):
+            for e in range(PACK):
                 nc.scalar.activation(
-                    out=t_plane[:, t, :],
-                    in_=z_banks[i][:, t, :],
+                    out=t_plane[:, e, :],
+                    in_=z_banks[i][:, e, :],
                     func=ACT.Gelu,
-                    scale=gain[:, t : t + 1],
-                    bias=shift[:, t : t + 1],
+                    scale=gain[:, e : e + 1],
+                    bias=shift[:, e : e + 1],
                 )
             t_planes[i] = t_plane
 
         def regroup_t(i):
             t_grouped = work.tile([P, P, PACK], BF16, align_bytes=64)
-            nc.vector.tensor_copy(out=t_grouped[:], in_=t_planes[i][:].rearrange("q t r -> q r t"))
+            nc.vector.tensor_copy(out=t_grouped[:], in_=t_planes[i][:].rearrange("q e r -> q r e"))
             t_words[i] = t_grouped
 
         def quantise_t(i):
@@ -277,15 +277,15 @@ def tile_liquidmemorycell_pa_kernel(
             nc.vector.quantize_mx(
                 out=t_codes[:].bitcast(FP8X4),
                 scales=t_scales[:],
-                in_=t_words[i][:].rearrange("q r t -> q (r t)"),
+                in_=t_words[i][:].rearrange("q r e -> q (r e)"),
             )
             t_mx[i] = (t_codes, t_scales)
 
         def second_matmul(i):
             t_codes, t_scales = t_mx[i]
-            acc2 = o_psum.tile([P, MEM], F32)
+            y_bank = y_psum.tile([P, MEM], F32)
             nc.tensor.matmul_mx(
-                out=acc2[:],
+                out=y_bank[:],
                 lhsT=t_codes[:].bitcast(FP8X4),
                 lhsT_scale=t_scales[:],
                 rhs=w2_codes[:].bitcast(FP8X4),
@@ -293,42 +293,35 @@ def tile_liquidmemorycell_pa_kernel(
                 start=True,
                 stop=True,
             )
-            o_banks[i] = acc2
+            y_banks[i] = y_bank
 
         def add_second_bias(i):
-            o = work.tile([P, MEM], F32)
-            nc.vector.tensor_tensor(out=o[:], in0=o_banks[i][:], in1=b2_rows[:], op=ALU.add)
-            o_rows[i] = o
+            y = work.tile([P, MEM], F32)
+            nc.vector.tensor_tensor(out=y[:], in0=y_banks[i][:], in1=b2_rows[:], op=ALU.add)
+            y_rows[i] = y
 
         def tanh_and_store(i):
-            nc.scalar.activation(out=o_rows[i][:], in_=o_rows[i][:], func=ACT.Tanh)
-            nc.sync.dma_start(out=out[i * P : (i + 1) * P, :], in_=o_rows[i][:])
+            nc.scalar.activation(out=y_rows[i][:], in_=y_rows[i][:], func=ACT.Tanh)
+            nc.sync.dma_start(out=out[i * P : (i + 1) * P, :], in_=y_rows[i][:])
 
         def run(stage, i, *half):
             if 0 <= i < ROW_TILES:
                 stage(i, *half)
 
-        def multiply(j):
-            run(second_matmul, j - 4)
-            run(first_matmul, j)
-
         def step(j):
-            multiply_first = j + 1 == TILES_BEFORE_W1
             run(load_rows, j + LOAD_AHEAD)
             run(add_bias_and_sum, j - 1)
             run(quantise_t, j - 4)
-            if multiply_first:
-                multiply(j)
             run(transpose_half, j + 1, 0)
             run(variance, j - 1)
             run(transpose_half, j + 1, 1)
             run(transpose_normalised, j - 3)
             run(sort_words, j + 2, 0)
             run(sort_words, j + 2, 1)
-            if not multiply_first:
-                multiply(j)
-            run(add_second_bias, j - 4)
+            run(second_matmul, j - 4)
+            run(first_matmul, j)
             run(normalise, j - 2)
+            run(add_second_bias, j - 4)
             run(quantise_half, j + 1, 0)
             run(gelu, j - 3)
             run(quantise_half, j + 1, 1)

@@ -26,10 +26,10 @@ ROW_TILES = B // P
 PASSES = DIN // K_PASS
 HALF_PASSES = PASSES // 2
 K_HALF = HALF_PASSES * K_PASS
+HALF_BANKS = 2
 BANK_PASSES = 2
 QUADRANTS = 4
 
-TILES_BEFORE_W1 = 2
 LOAD_AHEAD = 6
 
 FLOPS = 2 * B * DIN * F + 2 * B * F * MEM
@@ -44,6 +44,7 @@ def tile_liquidmemorycell_pa_kernel(
         const = ctx.enter_context(tc.tile_pool(name="const", bufs=1))
         raw_pool = ctx.enter_context(tc.tile_pool(name="raw", bufs=2 * LOAD_AHEAD))
         half_pool = ctx.enter_context(tc.tile_pool(name="half", bufs=4))
+        mx_pool = ctx.enter_context(tc.tile_pool(name="mx", bufs=6))
         work = ctx.enter_context(tc.tile_pool(name="work", bufs=3))
         stat = ctx.enter_context(tc.tile_pool(name="stat", bufs=4))
         c_psum = ctx.enter_context(tc.psum_pool(name="c_psum", bufs=4))
@@ -53,12 +54,8 @@ def tile_liquidmemorycell_pa_kernel(
 
         bias_row = const.tile([P, F + MEM], BF16)
         nc.vector.memset(bias_row[:], 0.0)
-        nc.scalar.dma_start(out=bias_row[0:1, 0:F], in_=b1.rearrange("(o f) -> o f", o=1))
-        nc.scalar.dma_start(out=bias_row[0:1, F : F + MEM], in_=b2.rearrange("(o f) -> o f", o=1))
         g1_bf = const.tile([P, PACK], BF16)
         be1_bf = const.tile([P, PACK], BF16)
-        nc.scalar.dma_start(out=g1_bf[:], in_=g1.rearrange("(q e) -> q e", e=PACK))
-        nc.scalar.dma_start(out=be1_bf[:], in_=be1.rearrange("(q e) -> q e", e=PACK))
 
         ones = const.tile([P, P], BF16)
         nc.vector.memset(ones[:], 1.0)
@@ -79,30 +76,40 @@ def tile_liquidmemorycell_pa_kernel(
 
         raw = {}
 
-        def load_rows(i):
+        def load_rows(i, pieces=1):
             rows = slice(i * P, (i + 1) * P)
+            width = K_HALF // pieces
             for s in range(2):
                 c_raw = raw_pool.tile([P, K_HALF], BF16)
+                raw[(i, s)] = c_raw
                 if s == 0:
                     nc.sync.dma_start(out=c_raw[:, 0:MEM], in_=h[rows, :])
-                    nc.sync.dma_start(out=c_raw[:, MEM:K_HALF], in_=x[rows, 0 : K_HALF - MEM])
-                else:
-                    nc.sync.dma_start(out=c_raw[:], in_=x[rows, K_HALF - MEM : IN_DIM])
-                raw[(i, s)] = c_raw
+                for n in range(pieces):
+                    start = max(n * width, MEM if s == 0 else 0)
+                    stop = (n + 1) * width
+                    first_column = s * K_HALF - MEM
+                    nc.sync.dma_start(
+                        out=c_raw[:, start:stop], in_=x[rows, first_column + start : first_column + stop]
+                    )
 
-        for i in range(TILES_BEFORE_W1):
-            load_rows(i)
+        load_rows(0, 2)
         for quad in range(QUADRANTS):
             nc.sync.dma_start(
                 out=w1_scales[32 * quad : 32 * quad + 4, :, :].bitcast(I32),
                 in_=W1_scales[:, 4 * quad : 4 * quad + 4, :].rearrange("g r n -> r g n").bitcast(I32),
             )
+        load_rows(1)
+        load_rows(2)
+        nc.sync.dma_start(out=bias_row[0:1, 0:F], in_=b1.rearrange("(o f) -> o f", o=1))
+        nc.sync.dma_start(out=bias_row[0:1, F : F + MEM], in_=b2.rearrange("(o f) -> o f", o=1))
         for g in range(PASSES):
             nc.sync.dma_start(
                 out=w1_codes[:, g, :].bitcast(I32),
                 in_=W1_words[g].rearrange("q n e -> q (n e)").bitcast(I32),
             )
-        for i in range(TILES_BEFORE_W1, LOAD_AHEAD - 2):
+        nc.sync.dma_start(out=g1_bf[:], in_=g1.rearrange("(q e) -> q e", e=PACK))
+        nc.sync.dma_start(out=be1_bf[:], in_=be1.rearrange("(q e) -> q e", e=PACK))
+        for i in range(3, LOAD_AHEAD - 1):
             load_rows(i)
         nc.sync.dma_start(
             out=w2_codes[:].bitcast(I32),
@@ -120,18 +127,17 @@ def tile_liquidmemorycell_pa_kernel(
         shift = const.tile([P, PACK], F32)
 
         def spread_small_vectors():
-            u_bank = u_psum.tile([P, F], F32)
-            nc.tensor.matmul(out=u_bank[:], lhsT=ones[:], rhs=bias_row[:, 0:F], start=True, stop=True)
-            nc.scalar.copy(out=b1_rows[:], in_=u_bank[:].rearrange("r (q e) -> r e q", e=PACK))
-            y_bank = y_psum.tile([P, MEM], F32)
+            z_bank = z_psum.tile([P, F], F32, tag="z_bank")
+            nc.tensor.matmul(out=z_bank[:], lhsT=ones[:], rhs=bias_row[:, 0:F], start=True, stop=True)
+            nc.scalar.copy(out=b1_rows[:], in_=z_bank[:].rearrange("r (q e) -> r e q", e=PACK))
+            y_bank = y_psum.tile([P, MEM], F32, tag="y_bank")
             nc.tensor.matmul(
                 out=y_bank[:], lhsT=ones[:], rhs=bias_row[:, F : F + MEM], start=True, stop=True
             )
             nc.scalar.copy(out=b2_rows[:], in_=y_bank[:])
-            nc.gpsimd.tensor_copy(out=gain[:], in_=g1_bf[:])
-            nc.gpsimd.tensor_copy(out=shift[:], in_=be1_bf[:])
 
         ordered = {}
+        c_banks = {}
         side_by_side = {}
         c_mx = {}
         u_banks = {}
@@ -147,34 +153,42 @@ def tile_liquidmemorycell_pa_kernel(
         y_banks = {}
         y_rows = {}
 
-        def sort_words(i, s):
+        def sort_words(i, s, pieces=1):
             c_sorted = half_pool.tile([P, HALF_PASSES, WORDS, P], F32)
-            nc.vector.tensor_copy(
-                out=c_sorted[:],
-                in_=raw[(i, s)][:]
-                .bitcast(F32)
-                .rearrange("r (g q w) -> r g w q", g=HALF_PASSES, w=WORDS),
-            )
+            count = HALF_PASSES // pieces
+            for n in range(pieces):
+                nc.vector.tensor_copy(
+                    out=c_sorted[:, n * count : (n + 1) * count, :, :],
+                    in_=raw[(i, s)][:, n * count * K_PASS : (n + 1) * count * K_PASS]
+                    .bitcast(F32)
+                    .rearrange("r (g q w) -> r g w q", g=count, w=WORDS),
+                )
             ordered[(i, s)] = c_sorted
 
-        def transpose_half(i, s):
-            grouped = half_pool.tile([P, HALF_PASSES, P, PACK], BF16, align_bytes=64)
-            for first in range(0, HALF_PASSES, BANK_PASSES):
-                c_bank = c_psum.tile([P, BANK_PASSES, WORDS, P], F32)
-                for g in range(BANK_PASSES):
-                    for w in range(WORDS):
-                        nc.tensor.transpose(
-                            c_bank[:, g, w, :], ordered[(i, s)][:, first + g, w, :], identity[:]
-                        )
-                nc.scalar.copy(
-                    out=grouped[:, first : first + BANK_PASSES, :, :].bitcast(F32),
-                    in_=c_bank[:].rearrange("q g w r -> q g r w"),
-                )
-            side_by_side[(i, s)] = grouped
+        def transpose_bank(i, n):
+            c_bank = c_psum.tile([P, BANK_PASSES, WORDS, P], F32, tag="c_bank")
+            c_banks[(i, n)] = c_bank
+            first = (n % HALF_BANKS) * BANK_PASSES
+            for g in range(BANK_PASSES):
+                for w in range(WORDS):
+                    nc.tensor.transpose(
+                        c_bank[:, g, w, :], ordered[(i, n // HALF_BANKS)][:, first + g, w, :], identity[:]
+                    )
+
+        def copy_bank(i, n):
+            s = n // HALF_BANKS
+            first = (n % HALF_BANKS) * BANK_PASSES
+            if first == 0:
+                grouped = half_pool.tile([P, HALF_PASSES, P, PACK], BF16, align_bytes=64)
+                side_by_side[(i, s)] = grouped
+            nc.scalar.copy(
+                out=side_by_side[(i, s)][:, first : first + BANK_PASSES, :, :].bitcast(F32),
+                in_=c_banks[(i, n)][:].rearrange("q g w r -> q g r w"),
+            )
 
         def quantise_half(i, s):
-            c_codes = half_pool.tile([P, HALF_PASSES, P], U32, align_bytes=64)
-            c_scales = half_pool.tile([P, HALF_PASSES, P], U8, align_bytes=64)
+            c_codes = mx_pool.tile([P, HALF_PASSES, P], U32, align_bytes=64)
+            c_scales = mx_pool.tile([P, HALF_PASSES, P], U8, align_bytes=64)
             nc.vector.quantize_mx(
                 out=c_codes[:].rearrange("q g r -> q (g r)").bitcast(FP8X4),
                 scales=c_scales[:].rearrange("q g r -> q (g r)"),
@@ -182,12 +196,14 @@ def tile_liquidmemorycell_pa_kernel(
             )
             c_mx[(i, s)] = (c_codes, c_scales)
 
-        def first_matmul(i):
-            u_bank = u_psum.tile([P, F], F32)
-            for g in range(PASSES):
+        def first_matmul(i, passes=range(PASSES)):
+            if i not in u_banks:
+                u_bank = u_psum.tile([P, F], F32)
+                u_banks[i] = u_bank
+            for g in passes:
                 c_codes, c_scales = c_mx[(i, g // HALF_PASSES)]
                 nc.tensor.matmul_mx(
-                    out=u_bank[:],
+                    out=u_banks[i][:],
                     lhsT=c_codes[:, g % HALF_PASSES, :].bitcast(FP8X4),
                     lhsT_scale=c_scales[:, g % HALF_PASSES, :],
                     rhs=w1_codes[:, g, :].bitcast(FP8X4),
@@ -195,7 +211,6 @@ def tile_liquidmemorycell_pa_kernel(
                     start=(g == 0),
                     stop=(g == PASSES - 1),
                 )
-            u_banks[i] = u_bank
 
         def add_bias_and_sum(i):
             u = work.tile([P, PACK, P], F32)
@@ -212,19 +227,21 @@ def tile_liquidmemorycell_pa_kernel(
             u_rows[i] = u
             row_sums[i] = row_sum
 
-        def variance(i):
+        def minus_mean(i):
             neg_mean = stat.tile([P, 1], F32)
             nc.vector.tensor_scalar(
                 out=neg_mean[:], in0=row_sums[i][:], scalar1=-1.0 / F, scalar2=None, op0=ALU.mult
             )
             neg_means[i] = neg_mean
+
+        def variance(i):
             squares = work.tile([P, F], BF16)
             sq_sum = stat.tile([P, 1], F32)
             nc.scalar.activation(
                 out=squares[:],
                 in_=u_rows[i][:].rearrange("r e q -> r (e q)"),
                 func=ACT.Square,
-                bias=neg_mean[:],
+                bias=neg_means[i][:],
                 scale=1.0,
                 accum_out=sq_sum[:],
             )
@@ -248,8 +265,8 @@ def tile_liquidmemorycell_pa_kernel(
             )
             z_rows[i] = z
 
-        def transpose_normalised(i):
-            z_bank = z_psum.tile([P, PACK, P], F32)
+        def transpose_normalised(i, pool=z_psum, tag="z_bank"):
+            z_bank = pool.tile([P, PACK, P], F32, tag=tag)
             for e in range(PACK):
                 nc.tensor.transpose(z_bank[:, e, :], z_rows[i][:, e, :], identity[:])
             z_banks[i] = z_bank
@@ -283,7 +300,7 @@ def tile_liquidmemorycell_pa_kernel(
 
         def second_matmul(i):
             t_codes, t_scales = t_mx[i]
-            y_bank = y_psum.tile([P, MEM], F32)
+            y_bank = y_psum.tile([P, MEM], F32, tag="y_bank")
             nc.tensor.matmul_mx(
                 out=y_bank[:],
                 lhsT=t_codes[:].bitcast(FP8X4),
@@ -309,27 +326,102 @@ def tile_liquidmemorycell_pa_kernel(
                 stage(i, *half)
 
         def step(j):
-            run(load_rows, j + LOAD_AHEAD)
-            run(add_bias_and_sum, j - 1)
-            run(quantise_t, j - 4)
-            run(transpose_half, j + 1, 0)
+            run(load_rows, j + LOAD_AHEAD - 1)
+            run(gelu, j - 3)
+            for n in range(4):
+                run(transpose_bank, j + 1, n)
+            run(minus_mean, j - 1)
+            run(add_second_bias, j - 4)
+            run(copy_bank, j + 1, 0)
+            run(copy_bank, j + 1, 1)
             run(variance, j - 1)
-            run(transpose_half, j + 1, 1)
-            run(transpose_normalised, j - 3)
+            run(regroup_t, j - 3)
+            run(copy_bank, j + 1, 2)
+            run(copy_bank, j + 1, 3)
             run(sort_words, j + 2, 0)
             run(sort_words, j + 2, 1)
-            run(second_matmul, j - 4)
+            run(quantise_t, j - 3)
             run(first_matmul, j)
+            run(second_matmul, j - 3)
             run(normalise, j - 2)
-            run(add_second_bias, j - 4)
+            run(transpose_normalised, j - 2)
             run(quantise_half, j + 1, 0)
-            run(gelu, j - 3)
             run(quantise_half, j + 1, 1)
             run(tanh_and_store, j - 4)
-            run(regroup_t, j - 3)
+            run(add_bias_and_sum, j)
 
-        step(-2)
-        step(-1)
+        def prepare(i):
+            for n in range(4):
+                transpose_bank(i, n)
+                copy_bank(i, n)
+
+        sort_words(0, 0, 2)
+        sort_words(0, 1, 2)
+        prepare(0)
+        quantise_half(0, 0)
+        sort_words(1, 0)
+        quantise_half(0, 1)
+        sort_words(1, 1)
+        prepare(1)
+        quantise_half(1, 0)
+        sort_words(2, 0)
+        quantise_half(1, 1)
+        sort_words(2, 1)
+        prepare(2)
+        quantise_half(2, 0)
+        quantise_half(2, 1)
         spread_small_vectors()
-        for j in range(ROW_TILES + 4):
+        load_rows(LOAD_AHEAD - 1)
+        load_rows(LOAD_AHEAD)
+        nc.gpsimd.tensor_copy(out=gain[:], in_=g1_bf[:])
+        nc.gpsimd.tensor_copy(out=shift[:], in_=be1_bf[:])
+        first_matmul(0)
+        first_matmul(1)
+        add_bias_and_sum(0)
+        minus_mean(0)
+        variance(0)
+        sort_words(3, 0)
+        sort_words(3, 1)
+        add_bias_and_sum(1)
+        for j in range(2, ROW_TILES - 1):
             step(j)
+
+        a, b, c, d = ROW_TILES - 4, ROW_TILES - 3, ROW_TILES - 2, ROW_TILES - 1
+        first_matmul(d)
+        gelu(a)
+        minus_mean(c)
+        add_second_bias(a - 1)
+        normalise(b)
+        transpose_normalised(b, c_psum, "c_bank")
+        variance(c)
+        tanh_and_store(a - 1)
+        regroup_t(a)
+        gelu(b)
+        quantise_t(a)
+        add_bias_and_sum(d)
+        minus_mean(d)
+        normalise(c)
+        transpose_normalised(c, c_psum, "c_bank")
+        second_matmul(a)
+        variance(d)
+        regroup_t(b)
+        add_second_bias(a)
+        quantise_t(b)
+        gelu(c)
+        second_matmul(b)
+        tanh_and_store(a)
+        normalise(d)
+        transpose_normalised(d, c_psum, "c_bank")
+        add_second_bias(b)
+        regroup_t(c)
+        gelu(d)
+        quantise_t(c)
+        second_matmul(c)
+        tanh_and_store(b)
+        regroup_t(d)
+        add_second_bias(c)
+        quantise_t(d)
+        second_matmul(d)
+        tanh_and_store(c)
+        add_second_bias(d)
+        tanh_and_store(d)

@@ -67,10 +67,10 @@ def tile_liquidmemorycell_pa_kernel(
         table_warmer = const.tile([P, 1], F32)
         nc.scalar.activation(out=table_warmer[:], in_=neg_half[:], func=ACT.Gelu)
 
-        w1_codes = const.tile([P, PASSES, PACK * F], U8, align_bytes=64)
-        w1_scales = const.tile([P, PASSES, F], U8, align_bytes=64)
-        w2_codes = const.tile([P, PACK * MEM], U8, align_bytes=64)
-        w2_scales = const.tile([P, MEM], U8, align_bytes=64)
+        w1_codes = const.tile([P, PASSES, PACK * F], U8, align_bytes=256)
+        w1_scales = const.tile([P, PASSES, F], U8, align_bytes=256)
+        w2_codes = const.tile([P, PACK * MEM], U8, align_bytes=256)
+        w2_scales = const.tile([P, MEM], U8, align_bytes=256)
         nc.vector.memset(w1_scales[:].bitcast(I32), 0)
         nc.vector.memset(w2_scales[:].bitcast(I32), 0)
 
@@ -179,7 +179,7 @@ def tile_liquidmemorycell_pa_kernel(
             s = n // HALF_BANKS
             first = (n % HALF_BANKS) * BANK_PASSES
             if first == 0:
-                grouped = half_pool.tile([P, HALF_PASSES, P, PACK], BF16, align_bytes=64)
+                grouped = half_pool.tile([P, HALF_PASSES, P, PACK], BF16, align_bytes=256)
                 side_by_side[(i, s)] = grouped
             nc.scalar.copy(
                 out=side_by_side[(i, s)][:, first : first + BANK_PASSES, :, :].bitcast(F32),
@@ -187,8 +187,8 @@ def tile_liquidmemorycell_pa_kernel(
             )
 
         def quantise_half(i, s):
-            c_codes = mx_pool.tile([P, HALF_PASSES, P], U32, align_bytes=64)
-            c_scales = mx_pool.tile([P, HALF_PASSES, P], U8, align_bytes=64)
+            c_codes = mx_pool.tile([P, HALF_PASSES, P], U32, align_bytes=256)
+            c_scales = mx_pool.tile([P, HALF_PASSES, P], U8, align_bytes=256)
             nc.vector.quantize_mx(
                 out=c_codes[:].rearrange("q g r -> q (g r)").bitcast(FP8X4),
                 scales=c_scales[:].rearrange("q g r -> q (g r)"),
@@ -284,13 +284,13 @@ def tile_liquidmemorycell_pa_kernel(
             t_planes[i] = t_plane
 
         def regroup_t(i):
-            t_grouped = work.tile([P, P, PACK], BF16, align_bytes=64)
+            t_grouped = work.tile([P, P, PACK], BF16, align_bytes=256)
             nc.vector.tensor_copy(out=t_grouped[:], in_=t_planes[i][:].rearrange("q e r -> q r e"))
             t_words[i] = t_grouped
 
         def quantise_t(i):
-            t_codes = work.tile([P, P], U32, align_bytes=64)
-            t_scales = work.tile([P, P], U8, align_bytes=64)
+            t_codes = work.tile([P, P], U32, align_bytes=256)
+            t_scales = work.tile([P, P], U8, align_bytes=256)
             nc.vector.quantize_mx(
                 out=t_codes[:].bitcast(FP8X4),
                 scales=t_scales[:],

@@ -46,11 +46,10 @@ def tile_liquidmemorycell_pa_kernel(
         half_pool = ctx.enter_context(tc.tile_pool(name="half", bufs=4))
         mx_pool = ctx.enter_context(tc.tile_pool(name="mx", bufs=6))
         work = ctx.enter_context(tc.tile_pool(name="work", bufs=3))
+        out_pool = ctx.enter_context(tc.tile_pool(name="out", bufs=5))
         stat = ctx.enter_context(tc.tile_pool(name="stat", bufs=4))
-        c_psum = ctx.enter_context(tc.psum_pool(name="c_psum", bufs=4))
         u_psum = ctx.enter_context(tc.psum_pool(name="u_psum", bufs=2))
-        z_psum = ctx.enter_context(tc.psum_pool(name="z_psum", bufs=1))
-        y_psum = ctx.enter_context(tc.psum_pool(name="y_psum", bufs=1))
+        psum = ctx.enter_context(tc.psum_pool(name="psum", bufs=6))
 
         bias_row = const.tile([P, F + MEM], BF16)
         nc.vector.memset(bias_row[:], 0.0)
@@ -59,13 +58,13 @@ def tile_liquidmemorycell_pa_kernel(
 
         ones = const.tile([P, P], BF16)
         nc.vector.memset(ones[:], 1.0)
-        neg_half = const.tile([P, 1], F32)
+        neg_half = const.tile([P, 2], F32)
         nc.vector.memset(neg_half[:], -0.5)
         identity = const.tile([P, P], F32)
         make_identity(nc, identity[:])
 
         table_warmer = const.tile([P, 1], F32)
-        nc.scalar.activation(out=table_warmer[:], in_=neg_half[:], func=ACT.Gelu)
+        nc.scalar.activation(out=table_warmer[:], in_=neg_half[:, 0:1], func=ACT.Gelu)
 
         w1_codes = const.tile([P, PASSES, PACK * F], U8, align_bytes=256)
         w1_scales = const.tile([P, PASSES, F], U8, align_bytes=256)
@@ -109,7 +108,7 @@ def tile_liquidmemorycell_pa_kernel(
             )
         nc.sync.dma_start(out=g1_bf[:], in_=g1.rearrange("(q e) -> q e", e=PACK))
         nc.sync.dma_start(out=be1_bf[:], in_=be1.rearrange("(q e) -> q e", e=PACK))
-        for i in range(3, LOAD_AHEAD - 1):
+        for i in range(3, LOAD_AHEAD):
             load_rows(i)
         nc.sync.dma_start(
             out=w2_codes[:].bitcast(I32),
@@ -122,19 +121,20 @@ def tile_liquidmemorycell_pa_kernel(
             )
 
         b1_rows = const.tile([P, PACK, P], F32)
-        b2_rows = const.tile([P, MEM], F32)
+        b2_rows = const.tile([P, 2, MEM], F32)
         gain = const.tile([P, PACK], F32)
         shift = const.tile([P, PACK], F32)
 
         def spread_small_vectors():
-            z_bank = z_psum.tile([P, F], F32, tag="z_bank")
-            nc.tensor.matmul(out=z_bank[:], lhsT=ones[:], rhs=bias_row[:, 0:F], start=True, stop=True)
-            nc.scalar.copy(out=b1_rows[:], in_=z_bank[:].rearrange("r (q e) -> r e q", e=PACK))
-            y_bank = y_psum.tile([P, MEM], F32, tag="y_bank")
-            nc.tensor.matmul(
-                out=y_bank[:], lhsT=ones[:], rhs=bias_row[:, F : F + MEM], start=True, stop=True
-            )
-            nc.scalar.copy(out=b2_rows[:], in_=y_bank[:])
+            bank = psum.tile([P, F], F32)
+            nc.tensor.matmul(out=bank[:], lhsT=ones[:], rhs=bias_row[:, 0:F], start=True, stop=True)
+            nc.scalar.copy(out=b1_rows[:], in_=bank[:].rearrange("r (q e) -> r e q", e=PACK))
+            bank = psum.tile([P, MEM], F32)
+            nc.tensor.matmul(out=bank[:], lhsT=ones[:], rhs=bias_row[:, F : F + MEM], start=True, stop=True)
+            for g in range(2):
+                nc.scalar.copy(out=b2_rows[:, g, :], in_=bank[:])
+            nc.gpsimd.tensor_copy(out=gain[:], in_=g1_bf[:])
+            nc.gpsimd.tensor_copy(out=shift[:], in_=be1_bf[:])
 
         ordered = {}
         c_banks = {}
@@ -154,6 +154,8 @@ def tile_liquidmemorycell_pa_kernel(
         y_rows = {}
 
         def sort_words(i, s, pieces=1):
+            if i >= ROW_TILES:
+                return
             c_sorted = half_pool.tile([P, HALF_PASSES, WORDS, P], F32)
             count = HALF_PASSES // pieces
             for n in range(pieces):
@@ -166,13 +168,13 @@ def tile_liquidmemorycell_pa_kernel(
             ordered[(i, s)] = c_sorted
 
         def transpose_bank(i, n):
-            c_bank = c_psum.tile([P, BANK_PASSES, WORDS, P], F32, tag="c_bank")
-            c_banks[(i, n)] = c_bank
+            bank = psum.tile([P, BANK_PASSES, WORDS, P], F32)
+            c_banks[(i, n)] = bank
             first = (n % HALF_BANKS) * BANK_PASSES
             for g in range(BANK_PASSES):
                 for w in range(WORDS):
                     nc.tensor.transpose(
-                        c_bank[:, g, w, :], ordered[(i, n // HALF_BANKS)][:, first + g, w, :], identity[:]
+                        bank[:, g, w, :], ordered[(i, n // HALF_BANKS)][:, first + g, w, :], identity[:]
                     )
 
         def copy_bank(i, n):
@@ -196,14 +198,13 @@ def tile_liquidmemorycell_pa_kernel(
             )
             c_mx[(i, s)] = (c_codes, c_scales)
 
-        def first_matmul(i, passes=range(PASSES)):
-            if i not in u_banks:
-                u_bank = u_psum.tile([P, F], F32)
-                u_banks[i] = u_bank
-            for g in passes:
+        def first_matmul(i):
+            u_bank = u_psum.tile([P, F], F32)
+            u_banks[i] = u_bank
+            for g in range(PASSES):
                 c_codes, c_scales = c_mx[(i, g // HALF_PASSES)]
                 nc.tensor.matmul_mx(
-                    out=u_banks[i][:],
+                    out=u_bank[:],
                     lhsT=c_codes[:, g % HALF_PASSES, :].bitcast(FP8X4),
                     lhsT_scale=c_scales[:, g % HALF_PASSES, :],
                     rhs=w1_codes[:, g, :].bitcast(FP8X4),
@@ -212,143 +213,139 @@ def tile_liquidmemorycell_pa_kernel(
                     stop=(g == PASSES - 1),
                 )
 
-        def add_bias_and_sum(i):
-            u = work.tile([P, PACK, P], F32)
-            row_sum = stat.tile([P, 1], F32)
+        def add_bias_and_sum(group, n):
+            if n == 0:
+                u = work.tile([P, len(group), PACK, P], F32)
+                row_sum = stat.tile([P, len(group)], F32)
+                u_rows[group] = u
+                row_sums[group] = row_sum
             nc.vector.scalar_tensor_tensor(
-                out=u[:],
-                in0=u_banks[i][:].rearrange("r (q e) -> r e q", e=PACK),
+                out=u_rows[group][:, n, :, :],
+                in0=u_banks[group[n]][:].rearrange("r (q e) -> r e q", e=PACK),
                 scalar=1.0,
                 in1=b1_rows[:],
                 op0=ALU.mult,
                 op1=ALU.add,
-                accum_out=row_sum[:],
+                accum_out=row_sums[group][:, n : n + 1],
             )
-            u_rows[i] = u
-            row_sums[i] = row_sum
 
-        def minus_mean(i):
-            neg_mean = stat.tile([P, 1], F32)
+        def minus_mean(group):
+            neg_mean = stat.tile([P, len(group)], F32)
             nc.vector.tensor_scalar(
-                out=neg_mean[:], in0=row_sums[i][:], scalar1=-1.0 / F, scalar2=None, op0=ALU.mult
+                out=neg_mean[:], in0=row_sums[group][:], scalar1=-1.0 / F, scalar2=None, op0=ALU.mult
             )
-            neg_means[i] = neg_mean
+            neg_means[group] = neg_mean
 
-        def variance(i):
-            squares = work.tile([P, F], BF16)
-            sq_sum = stat.tile([P, 1], F32)
-            nc.scalar.activation(
-                out=squares[:],
-                in_=u_rows[i][:].rearrange("r e q -> r (e q)"),
-                func=ACT.Square,
-                bias=neg_means[i][:],
-                scale=1.0,
-                accum_out=sq_sum[:],
-            )
-            var_eps = stat.tile([P, 1], F32)
+        def variance(group):
+            size = len(group)
+            sq_sum = stat.tile([P, size], F32)
+            for n in range(size):
+                squares = work.tile([P, F], BF16)
+                nc.scalar.activation(
+                    out=squares[:],
+                    in_=u_rows[group][:, n, :, :].rearrange("r e q -> r (e q)"),
+                    func=ACT.Square,
+                    bias=neg_means[group][:, n : n + 1],
+                    scale=1.0,
+                    accum_out=sq_sum[:, n : n + 1],
+                )
+            var_eps = stat.tile([P, size], F32)
             nc.gpsimd.tensor_scalar(
                 out=var_eps[:], in0=sq_sum[:], scalar1=1.0 / F, scalar2=LN_EPS, op0=ALU.mult, op1=ALU.add
             )
-            rstd = stat.tile([P, 1], F32)
-            nc.gpsimd.tensor_tensor(out=rstd[:], in0=var_eps[:], in1=neg_half[:], op=ALU.pow)
-            rstds[i] = rstd
+            rstd = stat.tile([P, size], F32)
+            nc.gpsimd.tensor_tensor(out=rstd[:], in0=var_eps[:], in1=neg_half[:, 0:size], op=ALU.pow)
+            rstds[group] = rstd
 
-        def normalise(i):
-            z = work.tile([P, PACK, P], F32)
-            nc.vector.tensor_scalar(
-                out=z[:],
-                in0=u_rows[i][:],
-                scalar1=neg_means[i][:],
-                scalar2=rstds[i][:],
-                op0=ALU.add,
-                op1=ALU.mult,
-            )
-            z_rows[i] = z
+        def normalise(group):
+            z = work.tile([P, len(group), PACK, P], F32)
+            for n in range(len(group)):
+                nc.vector.tensor_scalar(
+                    out=z[:, n, :, :],
+                    in0=u_rows[group][:, n, :, :],
+                    scalar1=neg_means[group][:, n : n + 1],
+                    scalar2=rstds[group][:, n : n + 1],
+                    op0=ALU.add,
+                    op1=ALU.mult,
+                )
+            z_rows[group] = z
 
-        def transpose_normalised(i, pool=z_psum, tag="z_bank"):
-            z_bank = pool.tile([P, PACK, P], F32, tag=tag)
-            for e in range(PACK):
-                nc.tensor.transpose(z_bank[:, e, :], z_rows[i][:, e, :], identity[:])
-            z_banks[i] = z_bank
+        def transpose_normalised(group):
+            size = len(group)
+            z_banks[group] = []
+            for b in range(size):
+                bank = psum.tile([P, PACK // size, size, P], F32)
+                z_banks[group].append(bank)
+                for k in range(PACK // size):
+                    for n in range(size):
+                        nc.tensor.transpose(
+                            bank[:, k, n, :], z_rows[group][:, n, b * (PACK // size) + k, :], identity[:]
+                        )
 
-        def gelu(i):
-            t_plane = work.tile([P, PACK, P], BF16)
+        def gelu(group):
+            size = len(group)
+            t_plane = work.tile([P, PACK, size, P], BF16)
             for e in range(PACK):
                 nc.scalar.activation(
-                    out=t_plane[:, e, :],
-                    in_=z_banks[i][:, e, :],
+                    out=t_plane[:, e, :, :],
+                    in_=z_banks[group][e * size // PACK][:, e % (PACK // size), :, :],
                     func=ACT.Gelu,
                     scale=gain[:, e : e + 1],
                     bias=shift[:, e : e + 1],
                 )
-            t_planes[i] = t_plane
+            t_planes[group] = t_plane
 
-        def regroup_t(i):
-            t_grouped = work.tile([P, P, PACK], BF16, align_bytes=256)
-            nc.vector.tensor_copy(out=t_grouped[:], in_=t_planes[i][:].rearrange("q e r -> q r e"))
-            t_words[i] = t_grouped
+        def regroup_t(group):
+            t_grouped = work.tile([P, len(group) * P, PACK], BF16, align_bytes=256)
+            nc.vector.tensor_copy(
+                out=t_grouped[:], in_=t_planes[group][:].rearrange("q e n r -> q (n r) e")
+            )
+            t_words[group] = t_grouped
 
-        def quantise_t(i):
-            t_codes = work.tile([P, P], U32, align_bytes=256)
-            t_scales = work.tile([P, P], U8, align_bytes=256)
+        def quantise_t(group):
+            t_codes = work.tile([P, len(group) * P], U32, align_bytes=256)
+            t_scales = work.tile([P, len(group) * P], U8, align_bytes=256)
             nc.vector.quantize_mx(
                 out=t_codes[:].bitcast(FP8X4),
                 scales=t_scales[:],
-                in_=t_words[i][:].rearrange("q r e -> q (r e)"),
+                in_=t_words[group][:].rearrange("q r e -> q (r e)"),
             )
-            t_mx[i] = (t_codes, t_scales)
+            t_mx[group] = (t_codes, t_scales)
 
-        def second_matmul(i):
-            t_codes, t_scales = t_mx[i]
-            y_bank = y_psum.tile([P, MEM], F32, tag="y_bank")
-            nc.tensor.matmul_mx(
-                out=y_bank[:],
-                lhsT=t_codes[:].bitcast(FP8X4),
-                lhsT_scale=t_scales[:],
-                rhs=w2_codes[:].bitcast(FP8X4),
-                rhs_scale=w2_scales[:],
-                start=True,
-                stop=True,
+        def second_matmul(group):
+            t_codes, t_scales = t_mx[group]
+            bank = psum.tile([P, len(group), MEM], F32)
+            for n in range(len(group)):
+                rows = slice(n * P, (n + 1) * P)
+                nc.tensor.matmul_mx(
+                    out=bank[:, n, :],
+                    lhsT=t_codes[:, rows].bitcast(FP8X4),
+                    lhsT_scale=t_scales[:, rows],
+                    rhs=w2_codes[:].bitcast(FP8X4),
+                    rhs_scale=w2_scales[:],
+                    start=True,
+                    stop=True,
+                )
+            y_banks[group] = bank
+
+        def add_second_bias(group):
+            y = out_pool.tile([P, len(group), MEM], F32)
+            nc.vector.tensor_tensor(
+                out=y[:], in0=y_banks[group][:], in1=b2_rows[:, 0 : len(group), :], op=ALU.add
             )
-            y_banks[i] = y_bank
+            y_rows[group] = y
 
-        def add_second_bias(i):
-            y = work.tile([P, MEM], F32)
-            nc.vector.tensor_tensor(out=y[:], in0=y_banks[i][:], in1=b2_rows[:], op=ALU.add)
-            y_rows[i] = y
+        def tanh_and_store(group):
+            nc.scalar.activation(out=y_rows[group][:], in_=y_rows[group][:], func=ACT.Tanh)
+            first = group[0] * P
+            nc.sync.dma_start(
+                out=out[first : first + len(group) * P, :].rearrange("(n r) m -> r n m", r=P),
+                in_=y_rows[group][:],
+            )
 
-        def tanh_and_store(i):
-            nc.scalar.activation(out=y_rows[i][:], in_=y_rows[i][:], func=ACT.Tanh)
-            nc.sync.dma_start(out=out[i * P : (i + 1) * P, :], in_=y_rows[i][:])
-
-        def run(stage, i, *half):
-            if 0 <= i < ROW_TILES:
-                stage(i, *half)
-
-        def step(j):
-            run(load_rows, j + LOAD_AHEAD - 1)
-            run(gelu, j - 3)
-            for n in range(4):
-                run(transpose_bank, j + 1, n)
-            run(minus_mean, j - 1)
-            run(add_second_bias, j - 4)
-            run(copy_bank, j + 1, 0)
-            run(copy_bank, j + 1, 1)
-            run(variance, j - 1)
-            run(regroup_t, j - 3)
-            run(copy_bank, j + 1, 2)
-            run(copy_bank, j + 1, 3)
-            run(sort_words, j + 2, 0)
-            run(sort_words, j + 2, 1)
-            run(quantise_t, j - 3)
-            run(first_matmul, j)
-            run(second_matmul, j - 3)
-            run(normalise, j - 2)
-            run(transpose_normalised, j - 2)
-            run(quantise_half, j + 1, 0)
-            run(quantise_half, j + 1, 1)
-            run(tanh_and_store, j - 4)
-            run(add_bias_and_sum, j)
+        def load(i):
+            if i < ROW_TILES:
+                load_rows(i)
 
         def prepare(i):
             for n in range(4):
@@ -371,57 +368,91 @@ def tile_liquidmemorycell_pa_kernel(
         quantise_half(2, 0)
         quantise_half(2, 1)
         spread_small_vectors()
-        load_rows(LOAD_AHEAD - 1)
-        load_rows(LOAD_AHEAD)
-        nc.gpsimd.tensor_copy(out=gain[:], in_=g1_bf[:])
-        nc.gpsimd.tensor_copy(out=shift[:], in_=be1_bf[:])
+        load(6)
+        load(7)
         first_matmul(0)
         first_matmul(1)
-        add_bias_and_sum(0)
-        minus_mean(0)
-        variance(0)
+        add_bias_and_sum((0,), 0)
+        minus_mean((0,))
+        variance((0,))
         sort_words(3, 0)
         sort_words(3, 1)
-        add_bias_and_sum(1)
-        for j in range(2, ROW_TILES - 1):
-            step(j)
+        load(8)
+        load(9)
+        add_bias_and_sum((1, 2), 0)
+        prepare(3)
+        sort_words(4, 0)
+        sort_words(4, 1)
+        first_matmul(2)
+        normalise((0,))
+        quantise_half(3, 0)
+        sort_words(5, 0)
+        quantise_half(3, 1)
+        sort_words(5, 1)
+        add_bias_and_sum((1, 2), 1)
+        def group_of(a):
+            return {-1: (0,), -3: None}.get(a, (a, a + 1))
+        for a in range(3, ROW_TILES - 1, 2):
+            new, gs, gz, gy = (a, a + 1), group_of(a - 2), group_of(a - 4), group_of(a - 6)
+            if a - 6 < -1: gy = None
+            load(a + 7)
+            load(a + 8)
+            minus_mean(gs)
+            prepare(a + 1)
+            prepare(a + 2)
+            transpose_normalised(gz)
+            if gy: quantise_t(gy)
+            sort_words(a + 3, 0)
+            quantise_half(a + 1, 0)
+            sort_words(a + 3, 1)
+            quantise_half(a + 1, 1)
+            first_matmul(a)
+            if gy: second_matmul(gy)
+            sort_words(a + 4, 0)
+            quantise_half(a + 2, 0)
+            if gy: add_second_bias(gy)
+            quantise_half(a + 2, 1)
+            first_matmul(a + 1)
+            variance(gs)
+            if gy: tanh_and_store(gy)
+            gelu(gz)
+            sort_words(a + 4, 1)
+            add_bias_and_sum(new, 0)
+            normalise(gs)
+            add_bias_and_sum(new, 1)
+            regroup_t(gz)
 
-        a, b, c, d = ROW_TILES - 4, ROW_TILES - 3, ROW_TILES - 2, ROW_TILES - 1
-        first_matmul(d)
-        gelu(a)
-        minus_mean(c)
-        add_second_bias(a - 1)
-        normalise(b)
-        transpose_normalised(b, c_psum, "c_bank")
-        variance(c)
-        tanh_and_store(a - 1)
-        regroup_t(a)
-        gelu(b)
-        quantise_t(a)
-        add_bias_and_sum(d)
-        minus_mean(d)
-        normalise(c)
-        transpose_normalised(c, c_psum, "c_bank")
-        second_matmul(a)
-        variance(d)
-        regroup_t(b)
-        add_second_bias(a)
-        quantise_t(b)
-        gelu(c)
-        second_matmul(b)
-        tanh_and_store(a)
-        normalise(d)
-        transpose_normalised(d, c_psum, "c_bank")
-        add_second_bias(b)
-        regroup_t(c)
-        gelu(d)
-        quantise_t(c)
-        second_matmul(c)
-        tanh_and_store(b)
-        regroup_t(d)
-        add_second_bias(c)
-        quantise_t(d)
-        second_matmul(d)
-        tanh_and_store(c)
-        add_second_bias(d)
-        tanh_and_store(d)
+        gf, gs, gz, gy = (15,), (13, 14), (11, 12), (9, 10)
+        first_matmul(15)
+        minus_mean(gs)
+        quantise_t(gy)
+        variance(gs)
+        second_matmul(gy)
+        transpose_normalised(gz)
+        add_bias_and_sum(gf, 0)
+        minus_mean(gf)
+        normalise(gs)
+        variance(gf)
+        transpose_normalised(gs)
+        gelu(gz)
+        add_second_bias(gy)
+        regroup_t(gz)
+        normalise(gf)
+        quantise_t(gz)
+        transpose_normalised(gf)
+        gelu(gs)
+        second_matmul(gz)
+        tanh_and_store(gy)
+        gelu(gf)
+        regroup_t(gs)
+        add_second_bias(gz)
+        quantise_t(gs)
+        regroup_t(gf)
+        second_matmul(gs)
+        quantise_t(gf)
+        second_matmul(gf)
+        tanh_and_store(gz)
+        add_second_bias(gs)
+        add_second_bias(gf)
+        tanh_and_store(gs)
+        tanh_and_store(gf)

@@ -144,6 +144,7 @@ def tile_liquidmemorycell_pa_kernel(
         u_rows = {}
         row_sums = {}
         neg_means = {}
+        sq_sums = {}
         rstds = {}
         z_rows = {}
         z_banks = {}
@@ -249,9 +250,13 @@ def tile_liquidmemorycell_pa_kernel(
                     scale=1.0,
                     accum_out=sq_sum[:, n : n + 1],
                 )
+            sq_sums[group] = sq_sum
+
+        def inverse_std(group):
+            size = len(group)
             var_eps = stat.tile([P, size], F32)
-            nc.gpsimd.tensor_scalar(
-                out=var_eps[:], in0=sq_sum[:], scalar1=1.0 / F, scalar2=LN_EPS, op0=ALU.mult, op1=ALU.add
+            nc.vector.tensor_scalar(
+                out=var_eps[:], in0=sq_sums[group][:], scalar1=1.0 / F, scalar2=LN_EPS, op0=ALU.mult, op1=ALU.add
             )
             rstd = stat.tile([P, size], F32)
             nc.gpsimd.tensor_tensor(out=rstd[:], in0=var_eps[:], in1=neg_half[:, 0:size], op=ALU.pow)
@@ -376,6 +381,7 @@ def tile_liquidmemorycell_pa_kernel(
         minus_mean((0,))
         variance((0,))
         sort_words(3, 0)
+        inverse_std((0,))
         sort_words(3, 1)
         load(8)
         load(9)
@@ -390,6 +396,7 @@ def tile_liquidmemorycell_pa_kernel(
         quantise_half(3, 1)
         sort_words(5, 1)
         add_bias_and_sum((1, 2), 1)
+
         def group_of(a):
             return {-1: (0,), -3: None}.get(a, (a, a + 1))
         for a in range(3, ROW_TILES - 1, 2):
@@ -399,28 +406,29 @@ def tile_liquidmemorycell_pa_kernel(
             load(a + 8)
             minus_mean(gs)
             prepare(a + 1)
-            prepare(a + 2)
-            transpose_normalised(gz)
+            variance(gs)
             if gy: quantise_t(gy)
             sort_words(a + 3, 0)
-            quantise_half(a + 1, 0)
             sort_words(a + 3, 1)
-            quantise_half(a + 1, 1)
+            quantise_half(a + 1, 0)
             first_matmul(a)
             if gy: second_matmul(gy)
-            sort_words(a + 4, 0)
-            quantise_half(a + 2, 0)
+            quantise_half(a + 1, 1)
+            prepare(a + 2)
             if gy: add_second_bias(gy)
-            quantise_half(a + 2, 1)
-            first_matmul(a + 1)
-            variance(gs)
-            if gy: tanh_and_store(gy)
-            gelu(gz)
+            transpose_normalised(gz)
+            sort_words(a + 4, 0)
+            inverse_std(gs)
             sort_words(a + 4, 1)
             add_bias_and_sum(new, 0)
             normalise(gs)
-            add_bias_and_sum(new, 1)
+            quantise_half(a + 2, 0)
+            gelu(gz)
+            quantise_half(a + 2, 1)
+            first_matmul(a + 1)
+            if gy: tanh_and_store(gy)
             regroup_t(gz)
+            add_bias_and_sum(new, 1)
 
         gf, gs, gz, gy = (15,), (13, 14), (11, 12), (9, 10)
         first_matmul(15)
@@ -431,16 +439,18 @@ def tile_liquidmemorycell_pa_kernel(
         transpose_normalised(gz)
         add_bias_and_sum(gf, 0)
         minus_mean(gf)
-        normalise(gs)
+        inverse_std(gs)
         variance(gf)
+        add_second_bias(gy)
+        normalise(gs)
+        inverse_std(gf)
         transpose_normalised(gs)
         gelu(gz)
-        add_second_bias(gy)
-        regroup_t(gz)
         normalise(gf)
-        quantise_t(gz)
+        regroup_t(gz)
         transpose_normalised(gf)
         gelu(gs)
+        quantise_t(gz)
         second_matmul(gz)
         tanh_and_store(gy)
         gelu(gf)

from contextlib import ExitStack

import concourse.mybir as mybir
from concourse.masks import make_identity

F32 = mybir.dt.float32
BF16 = mybir.dt.bfloat16
I32 = mybir.dt.int32
U32 = mybir.dt.uint32
U8 = mybir.dt.uint8
FP8X4 = mybir.dt.float8_e4m3fn_x4
ACT = mybir.ActivationFunctionType
ALU = mybir.AluOpType

P = 128
PACK = 4
WORDS = 2
K_PASS = P * PACK

B, IN_DIM, MEM = 2048, 3840, 256
DIN = MEM + IN_DIM
F = 2 * MEM
LN_EPS = 1e-5

ROW_TILES = B // P
PASSES = DIN // K_PASS
HALF_PASSES = PASSES // 2
K_HALF = HALF_PASSES * K_PASS
HALF_BANKS = 2
BANK_PASSES = 2
QUADRANTS = 4

LOAD_AHEAD = 6

FLOPS = 2 * B * DIN * F + 2 * B * F * MEM


def tile_liquidmemorycell_pa_kernel(
    tc, x, h, W1_words, W1_scales, b1, g1, be1, W2_words, W2_scales, b2, out
):
    nc = tc.nc
    with ExitStack() as ctx:
        ctx.enter_context(tc.manual_schedule())
        const = ctx.enter_context(tc.tile_pool(name="const", bufs=1))
        raw_pool = ctx.enter_context(tc.tile_pool(name="raw", bufs=2 * LOAD_AHEAD))
        half_pool = ctx.enter_context(tc.tile_pool(name="half", bufs=4))
        mx_pool = ctx.enter_context(tc.tile_pool(name="mx", bufs=6))
        work = ctx.enter_context(tc.tile_pool(name="work", bufs=3))
        out_pool = ctx.enter_context(tc.tile_pool(name="out", bufs=5))
        stat = ctx.enter_context(tc.tile_pool(name="stat", bufs=4))
        u_psum = ctx.enter_context(tc.psum_pool(name="u_psum", bufs=2))
        psum = ctx.enter_context(tc.psum_pool(name="psum", bufs=6))

        bias_row = const.tile([P, F + MEM], BF16)
        nc.vector.memset(bias_row[:], 0.0)
        g1_bf = const.tile([P, PACK], BF16)
        be1_bf = const.tile([P, PACK], BF16)

        ones = const.tile([P, P], BF16)
        nc.vector.memset(ones[:], 1.0)
        neg_half = const.tile([P, 2], F32)
        nc.vector.memset(neg_half[:], -0.5)
        identity = const.tile([P, P], F32)
        make_identity(nc, identity[:])

        table_warmer = const.tile([P, 1], F32)
        nc.scalar.activation(out=table_warmer[:], in_=neg_half[:, 0:1], func=ACT.Gelu)

        w1_codes = const.tile([P, PASSES, PACK * F], U8, align_bytes=256)
        w1_scales = const.tile([P, PASSES, F], U8, align_bytes=256)
        w2_codes = const.tile([P, PACK * MEM], U8, align_bytes=256)
        w2_scales = const.tile([P, MEM], U8, align_bytes=256)
        nc.vector.memset(w1_scales[:].bitcast(I32), 0)
        nc.vector.memset(w2_scales[:].bitcast(I32), 0)

        raw = {}

        def load_rows(i, pieces=1):
            rows = slice(i * P, (i + 1) * P)
            width = K_HALF // pieces
            for s in range(2):
                c_raw = raw_pool.tile([P, K_HALF], BF16)
                raw[(i, s)] = c_raw
                if s == 0:
                    nc.sync.dma_start(out=c_raw[:, 0:MEM], in_=h[rows, :])
                for n in range(pieces):
                    start = max(n * width, MEM if s == 0 else 0)
                    stop = (n + 1) * width
                    first_column = s * K_HALF - MEM
                    nc.sync.dma_start(
                        out=c_raw[:, start:stop], in_=x[rows, first_column + start : first_column + stop]
                    )

        load_rows(0, 2)
        for quad in range(QUADRANTS):
            nc.sync.dma_start(
                out=w1_scales[32 * quad : 32 * quad + 4, :, :].bitcast(I32),
                in_=W1_scales[:, 4 * quad : 4 * quad + 4, :].rearrange("g r n -> r g n").bitcast(I32),
            )
        load_rows(1)
        load_rows(2)
        nc.sync.dma_start(out=bias_row[0:1, 0:F], in_=b1.rearrange("(o f) -> o f", o=1))
        nc.sync.dma_start(out=bias_row[0:1, F : F + MEM], in_=b2.rearrange("(o f) -> o f", o=1))
        for g in range(PASSES):
            nc.sync.dma_start(
                out=w1_codes[:, g, :].bitcast(I32),
                in_=W1_words[g].rearrange("q n e -> q (n e)").bitcast(I32),
            )
        nc.sync.dma_start(out=g1_bf[:], in_=g1.rearrange("(q e) -> q e", e=PACK))
        nc.sync.dma_start(out=be1_bf[:], in_=be1.rearrange("(q e) -> q e", e=PACK))
        for i in range(3, LOAD_AHEAD):
            load_rows(i)
        nc.sync.dma_start(
            out=w2_codes[:].bitcast(I32),
            in_=W2_words[0].rearrange("q n e -> q (n e)").bitcast(I32),
        )
        for quad in range(QUADRANTS):
            nc.sync.dma_start(
                out=w2_scales[32 * quad : 32 * quad + 4, :].bitcast(I32),
                in_=W2_scales[0, 4 * quad : 4 * quad + 4, :].bitcast(I32),
            )

        b1_rows = const.tile([P, PACK, P], F32)
        b2_rows = const.tile([P, 2, MEM], F32)
        gain = const.tile([P, PACK], F32)
        shift = const.tile([P, PACK], F32)

        def spread_small_vectors():
            bank = psum.tile([P, F], F32)
            nc.tensor.matmul(out=bank[:], lhsT=ones[:], rhs=bias_row[:, 0:F], start=True, stop=True)
            nc.scalar.copy(out=b1_rows[:], in_=bank[:].rearrange("r (q e) -> r e q", e=PACK))
            bank = psum.tile([P, MEM], F32)
            nc.tensor.matmul(out=bank[:], lhsT=ones[:], rhs=bias_row[:, F : F + MEM], start=True, stop=True)
            for g in range(2):
                nc.scalar.copy(out=b2_rows[:, g, :], in_=bank[:])
            nc.gpsimd.tensor_copy(out=gain[:], in_=g1_bf[:])
            nc.gpsimd.tensor_copy(out=shift[:], in_=be1_bf[:])

        ordered = {}
        c_banks = {}
        side_by_side = {}
        c_mx = {}
        u_banks = {}
        u_rows = {}
        row_sums = {}
        neg_means = {}
        sq_sums = {}
        rstds = {}
        z_rows = {}
        z_banks = {}
        t_planes = {}
        t_words = {}
        t_mx = {}
        y_banks = {}
        y_rows = {}

        def sort_words(i, s, pieces=1):
            if i >= ROW_TILES:
                return
            c_sorted = half_pool.tile([P, HALF_PASSES, WORDS, P], F32)
            count = HALF_PASSES // pieces
            for n in range(pieces):
                nc.vector.tensor_copy(
                    out=c_sorted[:, n * count : (n + 1) * count, :, :],
                    in_=raw[(i, s)][:, n * count * K_PASS : (n + 1) * count * K_PASS]
                    .bitcast(F32)
                    .rearrange("r (g q w) -> r g w q", g=count, w=WORDS),
                )
            ordered[(i, s)] = c_sorted

        def transpose_bank(i, n):
            bank = psum.tile([P, BANK_PASSES, WORDS, P], F32)
            c_banks[(i, n)] = bank
            first = (n % HALF_BANKS) * BANK_PASSES
            for g in range(BANK_PASSES):
                for w in range(WORDS):
                    nc.tensor.transpose(
                        bank[:, g, w, :], ordered[(i, n // HALF_BANKS)][:, first + g, w, :], identity[:]
                    )

        def copy_bank(i, n):
            s = n // HALF_BANKS
            first = (n % HALF_BANKS) * BANK_PASSES
            if first == 0:
                grouped = half_pool.tile([P, HALF_PASSES, P, PACK], BF16, align_bytes=256)
                side_by_side[(i, s)] = grouped
            nc.scalar.copy(
                out=side_by_side[(i, s)][:, first : first + BANK_PASSES, :, :].bitcast(F32),
                in_=c_banks[(i, n)][:].rearrange("q g w r -> q g r w"),
            )

        def quantise_half(i, s):
            c_codes = mx_pool.tile([P, HALF_PASSES, P], U32, align_bytes=256)
            c_scales = mx_pool.tile([P, HALF_PASSES, P], U8, align_bytes=256)
            nc.vector.quantize_mx(
                out=c_codes[:].rearrange("q g r -> q (g r)").bitcast(FP8X4),
                scales=c_scales[:].rearrange("q g r -> q (g r)"),
                in_=side_by_side[(i, s)][:].rearrange("q g r e -> q (g r e)"),
            )
            c_mx[(i, s)] = (c_codes, c_scales)

        def first_matmul(i):
            u_bank = u_psum.tile([P, F], F32)
            u_banks[i] = u_bank
            for g in range(PASSES):
                c_codes, c_scales = c_mx[(i, g // HALF_PASSES)]
                nc.tensor.matmul_mx(
                    out=u_bank[:],
                    lhsT=c_codes[:, g % HALF_PASSES, :].bitcast(FP8X4),
                    lhsT_scale=c_scales[:, g % HALF_PASSES, :],
                    rhs=w1_codes[:, g, :].bitcast(FP8X4),
                    rhs_scale=w1_scales[:, g, :],
                    start=(g == 0),
                    stop=(g == PASSES - 1),
                )

        def add_bias_and_sum(group, n):
            if n == 0:
                u = work.tile([P, len(group), PACK, P], F32)
                row_sum = stat.tile([P, len(group)], F32)
                u_rows[group] = u
                row_sums[group] = row_sum
            nc.vector.scalar_tensor_tensor(
                out=u_rows[group][:, n, :, :],
                in0=u_banks[group[n]][:].rearrange("r (q e) -> r e q", e=PACK),
                scalar=1.0,
                in1=b1_rows[:],
                op0=ALU.mult,
                op1=ALU.add,
                accum_out=row_sums[group][:, n : n + 1],
            )

        def minus_mean(group):
            neg_mean = stat.tile([P, len(group)], F32)
            nc.vector.tensor_scalar(
                out=neg_mean[:], in0=row_sums[group][:], scalar1=-1.0 / F, scalar2=None, op0=ALU.mult
            )
            neg_means[group] = neg_mean

        def variance(group):
            size = len(group)
            sq_sum = stat.tile([P, size], F32)
            for n in range(size):
                squares = work.tile([P, F], BF16)
                nc.scalar.activation(
                    out=squares[:],
                    in_=u_rows[group][:, n, :, :].rearrange("r e q -> r (e q)"),
                    func=ACT.Square,
                    bias=neg_means[group][:, n : n + 1],
                    scale=1.0,
                    accum_out=sq_sum[:, n : n + 1],
                )
            sq_sums[group] = sq_sum

        def inverse_std(group):
            size = len(group)
            var_eps = stat.tile([P, size], F32)
            nc.vector.tensor_scalar(
                out=var_eps[:], in0=sq_sums[group][:], scalar1=1.0 / F, scalar2=LN_EPS, op0=ALU.mult, op1=ALU.add
            )
            rstd = stat.tile([P, size], F32)
            nc.gpsimd.tensor_tensor(out=rstd[:], in0=var_eps[:], in1=neg_half[:, 0:size], op=ALU.pow)
            rstds[group] = rstd

        def normalise(group):
            z = work.tile([P, len(group), PACK, P], F32)
            for n in range(len(group)):
                nc.vector.tensor_scalar(
                    out=z[:, n, :, :],
                    in0=u_rows[group][:, n, :, :],
                    scalar1=neg_means[group][:, n : n + 1],
                    scalar2=rstds[group][:, n : n + 1],
                    op0=ALU.add,
                    op1=ALU.mult,
                )
            z_rows[group] = z

        def transpose_normalised(group):
            size = len(group)
            z_banks[group] = []
            for b in range(size):
                bank = psum.tile([P, PACK // size, size, P], F32)
                z_banks[group].append(bank)
                for k in range(PACK // size):
                    for n in range(size):
                        nc.tensor.transpose(
                            bank[:, k, n, :], z_rows[group][:, n, b * (PACK // size) + k, :], identity[:]
                        )

        def gelu(group):
            size = len(group)
            t_plane = work.tile([P, PACK, size, P], BF16)
            for e in range(PACK):
                nc.scalar.activation(
                    out=t_plane[:, e, :, :],
                    in_=z_banks[group][e * size // PACK][:, e % (PACK // size), :, :],
                    func=ACT.Gelu,
                    scale=gain[:, e : e + 1],
                    bias=shift[:, e : e + 1],
                )
            t_planes[group] = t_plane

        def regroup_t(group):
            t_grouped = work.tile([P, len(group) * P, PACK], BF16, align_bytes=256)
            nc.vector.tensor_copy(
                out=t_grouped[:], in_=t_planes[group][:].rearrange("q e n r -> q (n r) e")
            )
            t_words[group] = t_grouped

        def quantise_t(group):
            t_codes = work.tile([P, len(group) * P], U32, align_bytes=256)
            t_scales = work.tile([P, len(group) * P], U8, align_bytes=256)
            nc.vector.quantize_mx(
                out=t_codes[:].bitcast(FP8X4),
                scales=t_scales[:],
                in_=t_words[group][:].rearrange("q r e -> q (r e)"),
            )
            t_mx[group] = (t_codes, t_scales)

        def second_matmul(group):
            t_codes, t_scales = t_mx[group]
            bank = psum.tile([P, len(group), MEM], F32)
            for n in range(len(group)):
                rows = slice(n * P, (n + 1) * P)
                nc.tensor.matmul_mx(
                    out=bank[:, n, :],
                    lhsT=t_codes[:, rows].bitcast(FP8X4),
                    lhsT_scale=t_scales[:, rows],
                    rhs=w2_codes[:].bitcast(FP8X4),
                    rhs_scale=w2_scales[:],
                    start=True,
                    stop=True,
                )
            y_banks[group] = bank

        def add_second_bias(group):
            y = out_pool.tile([P, len(group), MEM], F32)
            nc.vector.tensor_tensor(
                out=y[:], in0=y_banks[group][:], in1=b2_rows[:, 0 : len(group), :], op=ALU.add
            )
            y_rows[group] = y

        def tanh_and_store(group):
            nc.scalar.activation(out=y_rows[group][:], in_=y_rows[group][:], func=ACT.Tanh)
            first = group[0] * P
            nc.sync.dma_start(
                out=out[first : first + len(group) * P, :].rearrange("(n r) m -> r n m", r=P),
                in_=y_rows[group][:],
            )

        def load(i):
            if i < ROW_TILES:
                load_rows(i)

        def prepare(i):
            for n in range(4):
                transpose_bank(i, n)
                copy_bank(i, n)

        sort_words(0, 0, 2)
        sort_words(0, 1, 2)
        prepare(0)
        quantise_half(0, 0)
        sort_words(1, 0)
        quantise_half(0, 1)
        sort_words(1, 1)
        prepare(1)
        quantise_half(1, 0)
        sort_words(2, 0)
        quantise_half(1, 1)
        sort_words(2, 1)
        prepare(2)
        quantise_half(2, 0)
        quantise_half(2, 1)
        spread_small_vectors()
        load(6)
        load(7)
        first_matmul(0)
        first_matmul(1)
        add_bias_and_sum((0,), 0)
        minus_mean((0,))
        variance((0,))
        sort_words(3, 0)
        inverse_std((0,))
        sort_words(3, 1)
        load(8)
        load(9)
        add_bias_and_sum((1, 2), 0)
        prepare(3)
        sort_words(4, 0)
        sort_words(4, 1)
        first_matmul(2)
        normalise((0,))
        quantise_half(3, 0)
        sort_words(5, 0)
        quantise_half(3, 1)
        sort_words(5, 1)
        add_bias_and_sum((1, 2), 1)

        def group_of(a):
            return {-1: (0,), -3: None}.get(a, (a, a + 1))
        for a in range(3, ROW_TILES - 1, 2):
            new, gs, gz, gy = (a, a + 1), group_of(a - 2), group_of(a - 4), group_of(a - 6)
            if a - 6 < -1: gy = None
            load(a + 7)
            load(a + 8)
            minus_mean(gs)
            prepare(a + 1)
            variance(gs)
            if gy: quantise_t(gy)
            sort_words(a + 3, 0)
            sort_words(a + 3, 1)
            quantise_half(a + 1, 0)
            first_matmul(a)
            if gy: second_matmul(gy)
            quantise_half(a + 1, 1)
            prepare(a + 2)
            if gy: add_second_bias(gy)
            transpose_normalised(gz)
            sort_words(a + 4, 0)
            inverse_std(gs)
            sort_words(a + 4, 1)
            add_bias_and_sum(new, 0)
            normalise(gs)
            quantise_half(a + 2, 0)
            gelu(gz)
            quantise_half(a + 2, 1)
            first_matmul(a + 1)
            if gy: tanh_and_store(gy)
            regroup_t(gz)
            add_bias_and_sum(new, 1)

        gf, gs, gz, gy = (15,), (13, 14), (11, 12), (9, 10)
        first_matmul(15)
        minus_mean(gs)
        quantise_t(gy)
        variance(gs)
        second_matmul(gy)
        transpose_normalised(gz)
        add_bias_and_sum(gf, 0)
        minus_mean(gf)
        inverse_std(gs)
        variance(gf)
        add_second_bias(gy)
        normalise(gs)
        inverse_std(gf)
        transpose_normalised(gs)
        gelu(gz)
        normalise(gf)
        regroup_t(gz)
        transpose_normalised(gf)
        gelu(gs)
        quantise_t(gz)
        second_matmul(gz)
        tanh_and_store(gy)
        gelu(gf)
        regroup_t(gs)
        add_second_bias(gz)
        quantise_t(gs)
        regroup_t(gf)
        second_matmul(gs)
        quantise_t(gf)
        second_matmul(gf)
        tanh_and_store(gz)
        add_second_bias(gs)
        add_second_bias(gf)
        tanh_and_store(gs)
        tanh_and_store(gf)
